import numpy as np
import ml_dtypes

BF16 = ml_dtypes.bfloat16


def bf(x):
    return np.asarray(x, np.float32).astype(BF16)


def f32(x):
    return np.asarray(x, np.float32)


def f64(x):
    return np.asarray(x).astype(np.float64)


def striped(idx):
    return np.tile(idx.reshape(-1, 16).T, (8, 1))


D, V, S, N, GS = 256, 128, 2048, 512, 128
EPS = 1e-6


def setup_inputs():
    x = f32(np.random.standard_normal((D, N)) * (0.5 + 1.5 * np.random.random((1, N))))
    fn_w = f32(1.0 + 0.1 * np.random.standard_normal((D, 1)))
    lm_t = bf(np.random.choice([-1.0, 0.0, 1.0], size=(D, V)))
    lm_s = f32(np.random.uniform(0.03, 0.12, (V, D // GS)))
    base = f32(np.random.standard_normal((V, S)))
    return {"x": x, "fn_w": fn_w, "lm_t": lm_t, "lm_s": lm_s, "base": base, "offs": striped(np.random.permutation(S)[:N])}


def reference(x, fn_w, lm_t, lm_s, base, offs):
    idx = offs[:16].T.reshape(-1)
    w = f64(lm_t) * np.repeat(f64(lm_s).T, GS, axis=0)
    r = 1.0 / np.sqrt(np.mean(f64(x) ** 2, axis=0, keepdims=True) + EPS)
    y = w.T @ (f64(fn_w) * f64(x))
    out = f64(base).copy()
    out[:, idx] = y * r
    return out

@@ -1,0 +1,63 @@
+import concourse.mybir as mybir
+
+F32 = mybir.dt.float32
+BF16 = mybir.dt.bfloat16
+U16 = mybir.dt.uint16
+ALU = mybir.AluOpType
+ACT = mybir.ActivationFunctionType
+
+P = 128
+D = 256
+Q = D // P
+N = 512
+S = 2048
+EPS = 1e-6
+
+FLOPS = 2 * D * P * N + 2 * D * N
+
+
+def tile_lstetransformer_kernel(tc, x, fn_w, lm_t, lm_s, base, offs, out):
+    nc = tc.nc
+    with (
+        tc.tile_pool(name="held", bufs=1) as held,
+        tc.psum_pool(name="psum", bufs=1) as psum,
+    ):
+        x_blocks = [held.tile([P, N], F32, name=f"x{q}") for q in range(Q)]
+        for q in range(Q):
+            nc.sync.dma_start(x_blocks[q][:], x[q * P : (q + 1) * P, :])
+        offsets = held.tile([P, N // 16], U16, name="offsets")
+        nc.sync.dma_start(offsets[:], offs)
+        window = held.tile([P, S], F32, name="window")
+        nc.sync.dma_start(window[:], base)
+
+        gain = held.tile([P, Q], F32, name="gain")
+        with nc.allow_non_contiguous_dma(reason="one gain to a partition: 256 elements in all"):
+            nc.gpsimd.dma_start(gain[:], fn_w.rearrange("(q p) o -> p (q o)", p=P))
+        codes = held.tile([P, Q, P], BF16, name="codes")
+        nc.gpsimd.dma_start(codes[:], lm_t.rearrange("(q p) v -> p q v", p=P))
+        scales = held.tile([P, Q], F32, name="scales")
+        nc.gpsimd.dma_start(scales[:], lm_s)
+
+        ones = held.tile([P, P], BF16, name="ones")
+        nc.vector.memset(ones[:], 1.0)
+
+        logits = [psum.tile([P, N], F32, name=f"logits{q}") for q in range(Q)]
+        sum_squares = psum.tile([P, N], F32, name="sum_squares")
+        for q in range(Q):
+            h = held.tile([P, N], BF16, name=f"h{q}")
+            nc.vector.tensor_scalar_mul(h[:], x_blocks[q][:], gain[:, q : q + 1])
+            nc.tensor.matmul(logits[q][:], codes[:, q, :], h[:], start=True, stop=True)
+            squares = held.tile([P, N], BF16, name=f"squares{q}")
+            nc.scalar.activation(squares[:], x_blocks[q][:], ACT.Square)
+            nc.tensor.matmul(sum_squares[:], ones[:], squares[:], start=(q == 0), stop=(q == Q - 1))
+
+        r = held.tile([P, N], F32, name="r")
+        nc.scalar.activation(r[:], sum_squares[:], ACT.Abs_reciprocal_sqrt, bias=EPS, scale=1.0 / D)
+
+        y0 = held.tile([P, N], F32, name="y0")
+        nc.vector.tensor_scalar_mul(y0[:], logits[0][:], scales[:, 0:1])
+        y = held.tile([P, N], F32, name="y")
+        nc.vector.scalar_tensor_tensor(y[:], logits[1][:], scales[:, 1:2], y0[:], ALU.mult, ALU.add)
+
+        nc.vector.tensor_tensor(window[:].indirect(offsets[:]), y[:], r[:], ALU.mult)
+        nc.sync.dma_start(out, window[:])

@@ -22,21 +22,20 @@ def tile_lstetransformer_kernel(tc, x, fn_w, lm_t, lm_s, base, offs, out):
         tc.tile_pool(name="held", bufs=1) as held,
         tc.psum_pool(name="psum", bufs=1) as psum,
     ):
+        gain = held.tile([P, Q], F32, name="gain")
+        with nc.allow_non_contiguous_dma(reason="one gain to a partition: 256 elements in all"):
+            nc.sync.dma_start(gain[:], fn_w.rearrange("(q p) o -> p (q o)", p=P))
+        codes = held.tile([P, Q, P], BF16, name="codes")
+        nc.sync.dma_start(codes[:], lm_t.rearrange("(q p) v -> p q v", p=P))
         x_blocks = [held.tile([P, N], F32, name=f"x{q}") for q in range(Q)]
         for q in range(Q):
             nc.sync.dma_start(x_blocks[q][:], x[q * P : (q + 1) * P, :])
+        scales = held.tile([P, Q], F32, name="scales")
+        nc.sync.dma_start(scales[:], lm_s)
         offsets = held.tile([P, N // 16], U16, name="offsets")
         nc.sync.dma_start(offsets[:], offs)
         window = held.tile([P, S], F32, name="window")
         nc.sync.dma_start(window[:], base)
-
-        gain = held.tile([P, Q], F32, name="gain")
-        with nc.allow_non_contiguous_dma(reason="one gain to a partition: 256 elements in all"):
-            nc.gpsimd.dma_start(gain[:], fn_w.rearrange("(q p) o -> p (q o)", p=P))
-        codes = held.tile([P, Q, P], BF16, name="codes")
-        nc.gpsimd.dma_start(codes[:], lm_t.rearrange("(q p) v -> p q v", p=P))
-        scales = held.tile([P, Q], F32, name="scales")
-        nc.gpsimd.dma_start(scales[:], lm_s)
 
         ones = held.tile([P, P], BF16, name="ones")
         nc.vector.memset(ones[:], 1.0)

@@ -12,6 +12,7 @@ Q = D // P
 N = 512
 S = 2048
 EPS = 1e-6
+WARM_MATMULS = 4
 
 FLOPS = 2 * D * P * N + 2 * D * N
 
@@ -22,23 +23,33 @@ def tile_lstetransformer_kernel(tc, x, fn_w, lm_t, lm_s, base, offs, out):
         tc.tile_pool(name="held", bufs=1) as held,
         tc.psum_pool(name="psum", bufs=1) as psum,
     ):
-        gain = held.tile([P, Q], F32, name="gain")
-        with nc.allow_non_contiguous_dma(reason="one gain to a partition: 256 elements in all"):
-            nc.sync.dma_start(gain[:], fn_w.rearrange("(q p) o -> p (q o)", p=P))
-        codes = held.tile([P, Q, P], BF16, name="codes")
-        nc.sync.dma_start(codes[:], lm_t.rearrange("(q p) v -> p q v", p=P))
         x_blocks = [held.tile([P, N], F32, name=f"x{q}") for q in range(Q)]
         for q in range(Q):
             nc.sync.dma_start(x_blocks[q][:], x[q * P : (q + 1) * P, :])
-        scales = held.tile([P, Q], F32, name="scales")
-        nc.sync.dma_start(scales[:], lm_s)
         offsets = held.tile([P, N // 16], U16, name="offsets")
         nc.sync.dma_start(offsets[:], offs)
         window = held.tile([P, S], F32, name="window")
         nc.sync.dma_start(window[:], base)
 
+        gain = held.tile([P, Q], F32, name="gain")
+        with nc.allow_non_contiguous_dma(reason="one gain to a partition: 256 elements in all"):
+            nc.scalar.dma_start(gain[:], fn_w.rearrange("(q p) o -> p (q o)", p=P))
+        codes = held.tile([P, Q, P], BF16, name="codes")
+        nc.scalar.dma_start(codes[:], lm_t.rearrange("(q p) v -> p q v", p=P))
+        scales = held.tile([P, Q], F32, name="scales")
+        nc.scalar.dma_start(scales[:], lm_s)
+
         ones = held.tile([P, P], BF16, name="ones")
         nc.vector.memset(ones[:], 1.0)
+
+        scratch_column = held.tile([P, 1], F32, name="scratch_column")
+        nc.scalar.activation(scratch_column[:], ones[:, 0:1], ACT.Abs_reciprocal_sqrt)
+
+        zeros = held.tile([P, N], BF16, name="zeros")
+        nc.vector.memset(zeros[:], 0.0)
+        scratch_bank = psum.tile([P, N], F32, name="scratch_bank")
+        for i in range(WARM_MATMULS):
+            nc.tensor.matmul(scratch_bank[:], ones[:], zeros[:], start=True, stop=True)
 
         logits = [psum.tile([P, N], F32, name=f"logits{q}") for q in range(Q)]
         sum_squares = psum.tile([P, N], F32, name="sum_squares")

@@ -23,21 +23,20 @@ def tile_lstetransformer_kernel(tc, x, fn_w, lm_t, lm_s, base, offs, out):
         tc.tile_pool(name="held", bufs=1) as held,
         tc.psum_pool(name="psum", bufs=1) as psum,
     ):
+        gain = held.tile([P, Q], F32, name="gain")
+        with nc.allow_non_contiguous_dma(reason="one gain to a partition: 256 elements in all"):
+            nc.sync.dma_start(gain[:], fn_w.rearrange("(q p) o -> p (q o)", p=P))
+        codes = held.tile([P, Q, P], BF16, name="codes")
+        nc.sync.dma_start(codes[:], lm_t.rearrange("(q p) v -> p q v", p=P))
         x_blocks = [held.tile([P, N], F32, name=f"x{q}") for q in range(Q)]
         for q in range(Q):
             nc.sync.dma_start(x_blocks[q][:], x[q * P : (q + 1) * P, :])
+        scales = held.tile([P, Q], F32, name="scales")
+        nc.sync.dma_start(scales[:], lm_s)
         offsets = held.tile([P, N // 16], U16, name="offsets")
         nc.sync.dma_start(offsets[:], offs)
         window = held.tile([P, S], F32, name="window")
         nc.sync.dma_start(window[:], base)
-
-        gain = held.tile([P, Q], F32, name="gain")
-        with nc.allow_non_contiguous_dma(reason="one gain to a partition: 256 elements in all"):
-            nc.scalar.dma_start(gain[:], fn_w.rearrange("(q p) o -> p (q o)", p=P))
-        codes = held.tile([P, Q, P], BF16, name="codes")
-        nc.scalar.dma_start(codes[:], lm_t.rearrange("(q p) v -> p q v", p=P))
-        scales = held.tile([P, Q], F32, name="scales")
-        nc.scalar.dma_start(scales[:], lm_s)
 
         ones = held.tile([P, P], BF16, name="ones")
         nc.vector.memset(ones[:], 1.0)

@@ -11,6 +11,7 @@ D = 256
 Q = D // P
 N = 512
 S = 2048
+HALF = N // 2
 EPS = 1e-6
 WARM_MATMULS = 4
 
@@ -50,23 +51,25 @@ def tile_lstetransformer_kernel(tc, x, fn_w, lm_t, lm_s, base, offs, out):
         for i in range(WARM_MATMULS):
             nc.tensor.matmul(scratch_bank[:], ones[:], zeros[:], start=True, stop=True)
 
-        logits = [psum.tile([P, N], F32, name=f"logits{q}") for q in range(Q)]
-        sum_squares = psum.tile([P, N], F32, name="sum_squares")
+        halves = [slice(t * HALF, (t + 1) * HALF) for t in range(N // HALF)]
+        logits = [[psum.tile([P, HALF], F32, name=f"logits{q}_{t}") for t in range(len(halves))] for q in range(Q)]
+        sum_squares = [psum.tile([P, HALF], F32, name=f"sum_squares{t}") for t in range(len(halves))]
         for q in range(Q):
-            h = held.tile([P, N], BF16, name=f"h{q}")
-            nc.vector.tensor_scalar_mul(h[:], x_blocks[q][:], gain[:, q : q + 1])
-            nc.tensor.matmul(logits[q][:], codes[:, q, :], h[:], start=True, stop=True)
-            squares = held.tile([P, N], BF16, name=f"squares{q}")
-            nc.scalar.activation(squares[:], x_blocks[q][:], ACT.Square)
-            nc.tensor.matmul(sum_squares[:], ones[:], squares[:], start=(q == 0), stop=(q == Q - 1))
+            for t, half in enumerate(halves):
+                h = held.tile([P, HALF], BF16, name=f"h{q}_{t}")
+                nc.vector.tensor_scalar_mul(h[:], x_blocks[q][:, half], gain[:, q : q + 1])
+                nc.tensor.matmul(logits[q][t][:], codes[:, q, :], h[:], start=True, stop=True)
+                squares = held.tile([P, HALF], BF16, name=f"squares{q}_{t}")
+                nc.scalar.activation(squares[:], x_blocks[q][:, half], ACT.Square)
+                nc.tensor.matmul(sum_squares[t][:], ones[:], squares[:], start=(q == 0), stop=(q == Q - 1))
 
         r = held.tile([P, N], F32, name="r")
-        nc.scalar.activation(r[:], sum_squares[:], ACT.Abs_reciprocal_sqrt, bias=EPS, scale=1.0 / D)
-
-        y0 = held.tile([P, N], F32, name="y0")
-        nc.vector.tensor_scalar_mul(y0[:], logits[0][:], scales[:, 0:1])
         y = held.tile([P, N], F32, name="y")
-        nc.vector.scalar_tensor_tensor(y[:], logits[1][:], scales[:, 1:2], y0[:], ALU.mult, ALU.add)
+        for t, half in enumerate(halves):
+            nc.scalar.activation(r[:, half], sum_squares[t][:], ACT.Abs_reciprocal_sqrt, bias=EPS, scale=1.0 / D)
+            y0 = held.tile([P, HALF], F32, name=f"y0_{t}")
+            nc.vector.tensor_scalar_mul(y0[:], logits[0][t][:], scales[:, 0:1])
+            nc.vector.scalar_tensor_tensor(y[:, half], logits[1][t][:], scales[:, 1:2], y0[:], ALU.mult, ALU.add)
 
         nc.vector.tensor_tensor(window[:].indirect(offsets[:]), y[:], r[:], ALU.mult)
         nc.sync.dma_start(out, window[:])

@@ -60,7 +60,10 @@ def tile_lstetransformer_kernel(tc, x, fn_w, lm_t, lm_s, base, offs, out):
                 nc.vector.tensor_scalar_mul(h[:], x_blocks[q][:, half], gain[:, q : q + 1])
                 nc.tensor.matmul(logits[q][t][:], codes[:, q, :], h[:], start=True, stop=True)
                 squares = held.tile([P, HALF], BF16, name=f"squares{q}_{t}")
-                nc.scalar.activation(squares[:], x_blocks[q][:, half], ACT.Square)
+                if q == 0:
+                    nc.vector.tensor_tensor(squares[:], x_blocks[q][:, half], x_blocks[q][:, half], ALU.mult)
+                else:
+                    nc.scalar.activation(squares[:], x_blocks[q][:, half], ACT.Square)
                 nc.tensor.matmul(sum_squares[t][:], ones[:], squares[:], start=(q == 0), stop=(q == Q - 1))
 
         r = held.tile([P, N], F32, name="r")

@@ -60,19 +60,17 @@ def tile_lstetransformer_kernel(tc, x, fn_w, lm_t, lm_s, base, offs, out):
                 nc.vector.tensor_scalar_mul(h[:], x_blocks[q][:, half], gain[:, q : q + 1])
                 nc.tensor.matmul(logits[q][t][:], codes[:, q, :], h[:], start=True, stop=True)
                 squares = held.tile([P, HALF], BF16, name=f"squares{q}_{t}")
-                if q == 0:
-                    nc.vector.tensor_tensor(squares[:], x_blocks[q][:, half], x_blocks[q][:, half], ALU.mult)
-                else:
-                    nc.scalar.activation(squares[:], x_blocks[q][:, half], ACT.Square)
+                nc.scalar.activation(squares[:], x_blocks[q][:, half], ACT.Square)
                 nc.tensor.matmul(sum_squares[t][:], ones[:], squares[:], start=(q == 0), stop=(q == Q - 1))
 
         r = held.tile([P, N], F32, name="r")
         y = held.tile([P, N], F32, name="y")
+        y0 = [held.tile([P, HALF], F32, name=f"y0_{t}") for t in range(len(halves))]
+        nc.vector.tensor_scalar_mul(y0[0][:], logits[0][0][:], scales[:, 0:1])
+        nc.scalar.activation(y0[1][:], logits[0][1][:], ACT.Copy, scale=scales[:, 0:1])
         for t, half in enumerate(halves):
+            nc.vector.scalar_tensor_tensor(y[:, half], logits[1][t][:], scales[:, 1:2], y0[t][:], ALU.mult, ALU.add)
             nc.scalar.activation(r[:, half], sum_squares[t][:], ACT.Abs_reciprocal_sqrt, bias=EPS, scale=1.0 / D)
-            y0 = held.tile([P, HALF], F32, name=f"y0_{t}")
-            nc.vector.tensor_scalar_mul(y0[:], logits[0][t][:], scales[:, 0:1])
-            nc.vector.scalar_tensor_tensor(y[:, half], logits[1][t][:], scales[:, 1:2], y0[:], ALU.mult, ALU.add)
 
         nc.vector.tensor_tensor(window[:].indirect(offsets[:]), y[:], r[:], ALU.mult)
         nc.sync.dma_start(out, window[:])

@@ -12,6 +12,7 @@ Q = D // P
 N = 512
 S = 2048
 HALF = N // 2
+BLOCK = 32
 EPS = 1e-6
 WARM_MATMULS = 4
 
@@ -24,14 +25,18 @@ def tile_lstetransformer_kernel(tc, x, fn_w, lm_t, lm_s, base, offs, out):
         tc.tile_pool(name="held", bufs=1) as held,
         tc.psum_pool(name="psum", bufs=1) as psum,
     ):
-        gain = held.tile([P, Q], F32, name="gain")
-        with nc.allow_non_contiguous_dma(reason="one gain to a partition: 256 elements in all"):
-            nc.sync.dma_start(gain[:], fn_w.rearrange("(q p) o -> p (q o)", p=P))
+        gain_rows = held.tile([P, P], F32, name="gain_rows", align_bytes=64)
+        nc.gpsimd.memset(gain_rows[:], 0.0)
+
+        x_blocks = [held.tile([P, N], F32, name=f"x{q}") for q in range(Q)]
+        nc.sync.dma_start(x_blocks[0][:], x[0:P, :])
+        nc.sync.dma_start(
+            gain_rows[0:P:BLOCK, 0 : Q * BLOCK].rearrange("b (q f) -> b q f", q=Q),
+            fn_w.rearrange("(q b f) o -> b q (f o)", q=Q, f=BLOCK),
+        )
         codes = held.tile([P, Q, P], BF16, name="codes")
         nc.sync.dma_start(codes[:], lm_t.rearrange("(q p) v -> p q v", p=P))
-        x_blocks = [held.tile([P, N], F32, name=f"x{q}") for q in range(Q)]
-        for q in range(Q):
-            nc.sync.dma_start(x_blocks[q][:], x[q * P : (q + 1) * P, :])
+        nc.sync.dma_start(x_blocks[1][:], x[P : 2 * P, :])
         scales = held.tile([P, Q], F32, name="scales")
         nc.sync.dma_start(scales[:], lm_s)
         offsets = held.tile([P, N // 16], U16, name="offsets")
@@ -51,13 +56,16 @@ def tile_lstetransformer_kernel(tc, x, fn_w, lm_t, lm_s, base, offs, out):
         for i in range(WARM_MATMULS):
             nc.tensor.matmul(scratch_bank[:], ones[:], zeros[:], start=True, stop=True)
 
+        gain_columns = held.tile([P, P], F32, name="gain_columns", align_bytes=64)
+        nc.vector.transpose(gain_columns[:], gain_rows[:])
+
         halves = [slice(t * HALF, (t + 1) * HALF) for t in range(N // HALF)]
         logits = [[psum.tile([P, HALF], F32, name=f"logits{q}_{t}") for t in range(len(halves))] for q in range(Q)]
         sum_squares = [psum.tile([P, HALF], F32, name=f"sum_squares{t}") for t in range(len(halves))]
         for q in range(Q):
             for t, half in enumerate(halves):
                 h = held.tile([P, HALF], BF16, name=f"h{q}_{t}")
-                nc.vector.tensor_scalar_mul(h[:], x_blocks[q][:, half], gain[:, q : q + 1])
+                nc.vector.tensor_scalar_mul(h[:], x_blocks[q][:, half], gain_columns[:, q * BLOCK : q * BLOCK + 1])
                 nc.tensor.matmul(logits[q][t][:], codes[:, q, :], h[:], start=True, stop=True)
                 squares = held.tile([P, HALF], BF16, name=f"squares{q}_{t}")
                 nc.scalar.activation(squares[:], x_blocks[q][:, half], ACT.Square)

@@ -12,6 +12,7 @@ Q = D // P
 N = 512
 S = 2048
 HALF = N // 2
+DMA_LINE = 256
 BLOCK = 32
 EPS = 1e-6
 WARM_MATMULS = 4
@@ -28,20 +29,20 @@ def tile_lstetransformer_kernel(tc, x, fn_w, lm_t, lm_s, base, offs, out):
         gain_rows = held.tile([P, P], F32, name="gain_rows", align_bytes=64)
         nc.gpsimd.memset(gain_rows[:], 0.0)
 
-        x_blocks = [held.tile([P, N], F32, name=f"x{q}") for q in range(Q)]
+        x_blocks = [held.tile([P, N], F32, name=f"x{q}", align_bytes=DMA_LINE) for q in range(Q)]
         nc.sync.dma_start(x_blocks[0][:], x[0:P, :])
         nc.sync.dma_start(
             gain_rows[0:P:BLOCK, 0 : Q * BLOCK].rearrange("b (q f) -> b q f", q=Q),
             fn_w.rearrange("(q b f) o -> b q (f o)", q=Q, f=BLOCK),
         )
-        codes = held.tile([P, Q, P], BF16, name="codes")
+        codes = held.tile([P, Q, P], BF16, name="codes", align_bytes=DMA_LINE)
         nc.sync.dma_start(codes[:], lm_t.rearrange("(q p) v -> p q v", p=P))
         nc.sync.dma_start(x_blocks[1][:], x[P : 2 * P, :])
         scales = held.tile([P, Q], F32, name="scales")
         nc.sync.dma_start(scales[:], lm_s)
         offsets = held.tile([P, N // 16], U16, name="offsets")
         nc.sync.dma_start(offsets[:], offs)
-        window = held.tile([P, S], F32, name="window")
+        window = held.tile([P, S], F32, name="window", align_bytes=DMA_LINE)
         nc.sync.dma_start(window[:], base)
 
         ones = held.tile([P, P], BF16, name="ones")

import concourse.mybir as mybir

F32 = mybir.dt.float32
BF16 = mybir.dt.bfloat16
U16 = mybir.dt.uint16
ALU = mybir.AluOpType
ACT = mybir.ActivationFunctionType

P = 128
D = 256
Q = D // P
N = 512
S = 2048
HALF = N // 2
DMA_LINE = 256
BLOCK = 32
EPS = 1e-6
WARM_MATMULS = 4

FLOPS = 2 * D * P * N + 2 * D * N


def tile_lstetransformer_kernel(tc, x, fn_w, lm_t, lm_s, base, offs, out):
    nc = tc.nc
    with (
        tc.tile_pool(name="held", bufs=1) as held,
        tc.psum_pool(name="psum", bufs=1) as psum,
    ):
        gain_rows = held.tile([P, P], F32, name="gain_rows", align_bytes=64)
        nc.gpsimd.memset(gain_rows[:], 0.0)

        x_blocks = [held.tile([P, N], F32, name=f"x{q}", align_bytes=DMA_LINE) for q in range(Q)]
        nc.sync.dma_start(x_blocks[0][:], x[0:P, :])
        nc.sync.dma_start(
            gain_rows[0:P:BLOCK, 0 : Q * BLOCK].rearrange("b (q f) -> b q f", q=Q),
            fn_w.rearrange("(q b f) o -> b q (f o)", q=Q, f=BLOCK),
        )
        codes = held.tile([P, Q, P], BF16, name="codes", align_bytes=DMA_LINE)
        nc.sync.dma_start(codes[:], lm_t.rearrange("(q p) v -> p q v", p=P))
        nc.sync.dma_start(x_blocks[1][:], x[P : 2 * P, :])
        scales = held.tile([P, Q], F32, name="scales")
        nc.sync.dma_start(scales[:], lm_s)
        offsets = held.tile([P, N // 16], U16, name="offsets")
        nc.sync.dma_start(offsets[:], offs)
        window = held.tile([P, S], F32, name="window", align_bytes=DMA_LINE)
        nc.sync.dma_start(window[:], base)

        ones = held.tile([P, P], BF16, name="ones")
        nc.vector.memset(ones[:], 1.0)

        scratch_column = held.tile([P, 1], F32, name="scratch_column")
        nc.scalar.activation(scratch_column[:], ones[:, 0:1], ACT.Abs_reciprocal_sqrt)

        zeros = held.tile([P, N], BF16, name="zeros")
        nc.vector.memset(zeros[:], 0.0)
        scratch_bank = psum.tile([P, N], F32, name="scratch_bank")
        for i in range(WARM_MATMULS):
            nc.tensor.matmul(scratch_bank[:], ones[:], zeros[:], start=True, stop=True)

        gain_columns = held.tile([P, P], F32, name="gain_columns", align_bytes=64)
        nc.vector.transpose(gain_columns[:], gain_rows[:])

        halves = [slice(t * HALF, (t + 1) * HALF) for t in range(N // HALF)]
        logits = [[psum.tile([P, HALF], F32, name=f"logits{q}_{t}") for t in range(len(halves))] for q in range(Q)]
        sum_squares = [psum.tile([P, HALF], F32, name=f"sum_squares{t}") for t in range(len(halves))]
        for q in range(Q):
            for t, half in enumerate(halves):
                h = held.tile([P, HALF], BF16, name=f"h{q}_{t}")
                nc.vector.tensor_scalar_mul(h[:], x_blocks[q][:, half], gain_columns[:, q * BLOCK : q * BLOCK + 1])
                nc.tensor.matmul(logits[q][t][:], codes[:, q, :], h[:], start=True, stop=True)
                squares = held.tile([P, HALF], BF16, name=f"squares{q}_{t}")
                nc.scalar.activation(squares[:], x_blocks[q][:, half], ACT.Square)
                nc.tensor.matmul(sum_squares[t][:], ones[:], squares[:], start=(q == 0), stop=(q == Q - 1))

        r = held.tile([P, N], F32, name="r")
        y = held.tile([P, N], F32, name="y")
        y0 = [held.tile([P, HALF], F32, name=f"y0_{t}") for t in range(len(halves))]
        nc.vector.tensor_scalar_mul(y0[0][:], logits[0][0][:], scales[:, 0:1])
        nc.scalar.activation(y0[1][:], logits[0][1][:], ACT.Copy, scale=scales[:, 0:1])
        for t, half in enumerate(halves):
            nc.vector.scalar_tensor_tensor(y[:, half], logits[1][t][:], scales[:, 1:2], y0[t][:], ALU.mult, ALU.add)
            nc.scalar.activation(r[:, half], sum_squares[t][:], ACT.Abs_reciprocal_sqrt, bias=EPS, scale=1.0 / D)

        nc.vector.tensor_tensor(window[:].indirect(offsets[:]), y[:], r[:], ALU.mult)
        nc.sync.dma_start(out, window[:])
